import numpy as np
import ml_dtypes


def mxq(x, axis, fmt="e4m3"):
    dtype, down = {"e4m3": (ml_dtypes.float8_e4m3fn, 7), "e5m2": (ml_dtypes.float8_e5m2, 14)}[fmt]
    v = np.moveaxis(np.asarray(x, np.float32).astype(ml_dtypes.bfloat16).astype(np.float64), axis, -1)
    blocks = v.reshape(v.shape[:-1] + (-1, 32))
    amax = np.abs(blocks).max(-1, keepdims=True)
    byte = np.maximum(np.where(amax > 0, np.frexp(amax)[1] - 1 + 127, 0) - down, 1)
    scale = np.exp2(byte - 127.0)
    codes = (blocks / scale).astype(np.float32).astype(dtype).astype(np.float64)
    return np.moveaxis((codes * scale).reshape(v.shape), -1, axis)


WIDE = False


def mx_kscale(k):
    if not WIDE:
        return np.ones(k)
    levels = np.array([10, -10, 5, -5, 0])
    if k % 512:
        return np.exp2(np.random.permutation(np.resize(levels, k // 32))).repeat(32)
    a = np.empty((k // 512, 16))
    for p in range(k // 512):
        a[p, :8] = np.random.permutation(np.resize(levels, 8))
        for g in range(8):
            far = levels[np.abs(levels - a[p, g]) >= 10]
            a[p, g + 8] = far[np.random.randint(len(far))]
    return np.exp2(a.ravel()).repeat(32)


BF16 = ml_dtypes.bfloat16


def bf(x):
    return np.asarray(x, np.float32).astype(BF16)


def f64(x):
    return np.asarray(x).astype(np.float64)


B, D_IN, D_H, W_RANK, U_RANK = 1024, 1024, 2048, 512, 512


def sigmoid(v):
    return 1.0 / (1.0 + np.exp(-v))


def setup_inputs():
    s, t = mx_kscale(W_RANK), mx_kscale(U_RANK)
    return {
        "wx_r": bf(np.random.standard_normal((B, W_RANK)) * s),
        "uh_r": bf(np.random.standard_normal((B, U_RANK)) * t),
        "state": bf(np.random.standard_normal((B, D_H))),
        "W2": bf(np.random.standard_normal((D_H, W_RANK)) * 0.7 / np.sqrt(W_RANK) / s),
        "U2": bf(np.random.standard_normal((D_H, U_RANK)) * 0.7 / np.sqrt(U_RANK) / t),
        "bias_gate": bf(1.0 + 0.5 * np.random.standard_normal((1, D_H))),
        "bias_update": bf(1.0 + 0.5 * np.random.standard_normal((1, D_H))),
        "zeta": bf(1.0 + 0.1 * np.random.standard_normal((1, 1))),
        "nu": bf(-1.5 + 0.1 * np.random.standard_normal((1, 1))),
    }


def core(wx_r, uh_r, state, W2, U2, bias_gate, bias_update, zeta, nu):
    wx = mxq(f64(wx_r), 1, "e4m3") @ mxq(f64(W2), 1, "e4m3").T
    uh = mxq(f64(uh_r), 1, "e4m3") @ mxq(f64(U2), 1, "e4m3").T
    pre = wx + uh
    z = sigmoid(pre + f64(bias_gate))
    h_cand = np.tanh(pre + f64(bias_update))
    return z * f64(state) + (sigmoid(f64(zeta)) * (1.0 - z) + sigmoid(f64(nu))) * h_cand


def e4m3fn_bytes(y):
    return np.clip(np.asarray(y, np.float64), -448.0, 448.0).astype(np.float32).astype(ml_dtypes.float8_e4m3fn).view(np.uint8)


def reference(wx_r, uh_r, state, W2, U2, bias_gate, bias_update, zeta, nu):
    out = core(wx_r, uh_r, state, W2, U2, bias_gate, bias_update, zeta, nu)
    s = np.max(np.abs(out), axis=-1, keepdims=True) / 448.0
    return out, e4m3fn_bytes(out / s)

@@ -1,0 +1,434 @@
+from contextlib import ExitStack
+
+import concourse.mybir as mybir
+from concourse.masks import make_identity
+
+B, DH, RANK = 1024, 2048, 512
+FLOPS = 2 * B * DH * 2 * RANK
+
+F32 = mybir.dt.float32
+BF16 = mybir.dt.bfloat16
+U32 = mybir.dt.uint32
+U8 = mybir.dt.uint8
+FP8X4 = mybir.dt.float8_e4m3fn_x4
+FP8 = mybir.dt.float8_e4m3fn
+ACT = mybir.ActivationFunctionType
+ALU = mybir.AluOpType
+AX = mybir.AxisListType
+
+P = 128
+NJ = 8
+NDT = 16
+CH = 512
+NU = 32
+LOOK = 3
+LOOK_LATE = 4
+LATE = 12
+XFROM = 10
+BATCHES = [[i] for i in range(12)] + [[i, i + 1] for i in range(12, 30, 2)] + [[30], [31]]
+CAST0 = 23
+VEVAC = 20
+NPART = 5
+VCAST = 1280
+
+
+def tile_fastgrnncudacell_pa_kernel(
+    tc, wx_r, uh_r, state, W2, U2, bias_gate, bias_update, zeta, nu, out_0, out_1
+):
+    nc = tc.nc
+    with ExitStack() as ctx:
+        const = ctx.enter_context(tc.tile_pool(name="const", bufs=1))
+        rawp = ctx.enter_context(tc.tile_pool(name="rawp", bufs=6))
+        keep = ctx.enter_context(tc.tile_pool(name="keep", bufs=1))
+        grp = ctx.enter_context(tc.tile_pool(name="grp", bufs=2))
+        work = ctx.enter_context(tc.tile_pool(name="work", bufs=4))
+        psa = ctx.enter_context(tc.psum_pool(name="psa", bufs=2))
+        pst = ctx.enter_context(tc.psum_pool(name="pst", bufs=6))
+        ctx.enter_context(tc.manual_schedule())
+
+        x_views = [a.rearrange("(p j) k -> p j k", j=NJ) for a in (wx_r, uh_r)]
+        w_views = [a.rearrange("(t m) k -> m t k", m=P) for a in (W2, U2)]
+        st_view = state.rearrange("(p j) d -> p j d", j=NJ)
+        o0_view = out_0.rearrange("(p j) d -> p j d", j=NJ)
+        o1_view = out_1.rearrange("(p j) d -> p j d", j=NJ)
+
+        brow = const.tile([P, P], BF16, name="brow", tag="brow")
+        nc.vector.memset(brow[:], 0.0)
+        zt = const.tile([P, 1], BF16, name="zt", tag="zt")
+        nt = const.tile([P, 1], BF16, name="nt", tag="nt")
+        nc.scalar.dma_start(out=zt[:], in_=zeta.to_broadcast([P, 1]))
+        nc.scalar.dma_start(out=nt[:], in_=nu.to_broadcast([P, 1]))
+        nc.scalar.dma_start(out=brow[0:NDT, :], in_=bias_gate.rearrange("o (t m) -> (o t) m", m=P))
+        nc.scalar.dma_start(out=brow[NDT : 2 * NDT, :], in_=bias_update.rearrange("o (t m) -> (o t) m", m=P))
+
+        ST = [keep.tile([P, 4, DH], BF16, name="st%d" % c, tag="st%d" % c) for c in range(2)]
+        OT = [keep.tile([P, 4, DH], F32, name="ot%d" % c, tag="ot%d" % c) for c in range(2)]
+
+        def load_x(c):
+            res = []
+            for op in range(2):
+                r = rawp.tile([P, 4, RANK], BF16, name="raw", tag="raw")
+                nc.sync.dma_start(out=r[:], in_=x_views[op][:, 4 * c : 4 * c + 4, :])
+                res.append(r)
+            return res
+
+        def load_wg(g):
+            res = []
+            for op in range(2):
+                r = rawp.tile([P, 4, RANK], BF16, name="raw", tag="raw")
+                nc.sync.dma_start(out=r[:], in_=w_views[op][:, 4 * g : 4 * g + 4, :])
+                res.append(r)
+            return res
+
+        def load_state(c, a, b):
+            nc.sync.dma_start(out=ST[c][:, :, a:b], in_=st_view[:, 4 * c : 4 * c + 4, a:b])
+
+        rx0 = load_x(0)
+        rw0 = {}
+        for dt in range(4):
+            for op in range(2):
+                r = keep.tile([P, RANK], BF16, name="rw%d%d" % (dt, op), tag="rw%d%d" % (dt, op))
+                nc.sync.dma_start(out=r[:], in_=w_views[op][:, dt, :])
+                rw0[(dt, op)] = r
+        rwg = {}
+        rwg[1] = load_wg(1)
+        load_state(0, 0, CH)
+        load_state(0, CH, 2 * CH)
+        rwg[2] = load_wg(2)
+        load_state(0, 2 * CH, 3 * CH)
+
+        ident = const.tile([P, P], F32, name="ident", tag="ident")
+        make_identity(nc, ident[:])
+        identb = const.tile([P, P], BF16, name="identb", tag="identb")
+        make_identity(nc, identb[:])
+        zero = const.tile([P, 1], F32, name="zero", tag="zero")
+        nc.vector.memset(zero[:], 0.0)
+        am = const.tile([P, 2 * 4 * NPART], F32, name="am", tag="am")
+        nc.vector.memset(am[:], 0.0)
+        fac = const.tile([P, 3, 8], F32, name="fac", tag="fac")
+        sg = const.tile([P, 2], F32, name="sg", tag="sg")
+        nc.scalar.activation(out=sg[:, 0:1], in_=zt[:], func=ACT.Sigmoid)
+        nc.scalar.activation(out=sg[:, 1:2], in_=nt[:], func=ACT.Sigmoid)
+        cst = const.tile([P, 2], F32, name="cst", tag="cst")
+        brow32 = const.tile([P, P], F32, name="brow32", tag="brow32")
+        nc.vector.tensor_copy(out=brow32[:], in_=brow[:])
+        bias = const.tile([P, 2 * NDT], F32, name="bias", tag="bias")
+
+        wloc = {}
+        xloc = {}
+
+        def new_job(name, srcs, big):
+            n = len(srcs)
+            codes = keep.tile([P, n * P], U32, name="c" + name, tag="c" + name, align_bytes=64)
+            scales = keep.tile([P, n * P], U8, name="s" + name, tag="s" + name, align_bytes=64)
+            gtag = "grL" if big else "grS"
+            grouped = grp.tile([P, n * P * 4], BF16, name=gtag, tag=gtag, align_bytes=64, bufs=(1 if big else 2))
+            g32 = grouped[:].bitcast(F32).rearrange("p (s r u) -> p s r u", s=n, u=2)
+            return {"srcs": srcs, "codes": codes, "scales": scales, "grouped": grouped, "g32": g32}
+
+        def piece(job, k, eng):
+            bank = pst.tile([P, 2, 2, P], F32, name="tp", tag="tp")
+            for s in range(2):
+                words = job["srcs"][2 * k + s].bitcast(F32)
+                for u in range(2):
+                    nc.tensor.transpose(bank[:, s, u, :], words[:, u : RANK // 2 : 2], ident[:])
+            src = bank[:].rearrange("p s u r -> p s r u")
+            dst = job["g32"][:, 2 * k : 2 * k + 2]
+            if eng == "v":
+                nc.vector.tensor_copy(out=dst, in_=src)
+            else:
+                nc.scalar.copy(out=dst, in_=src)
+
+        def quant(job):
+            nc.vector.quantize_mx(
+                out=job["codes"][:].bitcast(FP8X4), scales=job["scales"][:], in_=job["grouped"][:]
+            )
+
+        def w_job(name, dts, big):
+            srcs = []
+            for dt in dts:
+                for op in range(2):
+                    if dt < 4:
+                        srcs.append(rw0[(dt, op)][:])
+                    else:
+                        srcs.append(rwg[dt // 4][op][:, dt % 4, :])
+            job = new_job(name, srcs, big)
+            for n, dt in enumerate(dts):
+                for op in range(2):
+                    wloc[(dt, op)] = (job, (2 * n + op) * P)
+            return job
+
+        def x_job(name, c, raws, ops, big):
+            srcs = []
+            for op in ops:
+                for jj in range(4):
+                    srcs.append(raws[op][:, jj, :])
+            job = new_job(name, srcs, big)
+            for n, op in enumerate(ops):
+                xloc[(c, op)] = (job, n * CH)
+            return job
+
+        accs = {}
+        zs = {}
+        qs = {}
+        zTs = {}
+        qTs = {}
+
+        def mx(i):
+            c, dt = i // NDT, i % NDT
+            acc = psa.tile([P, CH], F32, name="acc", tag="acc")
+            for op in range(2):
+                wj, wo = wloc[(dt, op)]
+                xj, xo = xloc[(c, op)]
+                nc.tensor.matmul_mx(
+                    out=acc[:],
+                    lhsT=wj["codes"][:, wo : wo + P].bitcast(FP8X4),
+                    lhsT_scale=wj["scales"][:, wo : wo + P],
+                    rhs=xj["codes"][:, xo : xo + CH].bitcast(FP8X4),
+                    rhs_scale=xj["scales"][:, xo : xo + CH],
+                    start=(op == 0),
+                    stop=(op == 1),
+                )
+            accs[i] = acc
+
+        batch_of = {}
+        for units in BATCHES:
+            for i in units:
+                batch_of[i] = units
+        zb = {}
+        qb = {}
+
+        def act(i):
+            dt = i % NDT
+            units = batch_of[i]
+            if i == units[0]:
+                zb[i] = work.tile([P, len(units), CH], F32, name="z", tag="z")
+                qb[i] = work.tile([P, len(units), CH], F32, name="q", tag="q")
+            k = i - units[0]
+            zs[i] = zb[units[0]][:, k, :]
+            qs[i] = qb[units[0]][:, k, :]
+            nc.scalar.activation(out=zs[i], in_=accs[i][:], func=ACT.Sigmoid, bias=bias[:, dt : dt + 1], scale=1.0)
+            nc.scalar.activation(
+                out=qs[i], in_=accs[i][:], func=ACT.Tanh, bias=bias[:, NDT + dt : NDT + dt + 1], scale=1.0
+            )
+
+        def gq(i):
+            units = batch_of[i]
+            if i != units[-1]:
+                return
+            z, q = zb[units[0]], qb[units[0]]
+            gt = work.tile([P, len(units), CH], F32, name="gt", tag="gt", bufs=2)
+            nc.gpsimd.tensor_scalar(
+                out=gt[:], in0=z[:], scalar1=cst[:, 0:1], scalar2=cst[:, 1:2], op0=ALU.mult, op1=ALU.add
+            )
+            nc.gpsimd.tensor_tensor(out=q[:], in0=gt[:], in1=q[:], op=ALU.mult)
+
+        def tt(i):
+            zT = pst.tile([P, 4, P], F32, name="tp", tag="tp")
+            qT = pst.tile([P, 4, P], F32, name="tp", tag="tp")
+            for jj in range(4):
+                nc.tensor.transpose(zT[:, jj, :], zs[i][:, jj * P : (jj + 1) * P], ident[:])
+            for jj in range(4):
+                nc.tensor.transpose(qT[:, jj, :], qs[i][:, jj * P : (jj + 1) * P], ident[:])
+            zTs[i] = zT
+            qTs[i] = qT
+
+        def vv(i):
+            c, dt = i // NDT, i % NDT
+            cols = slice(dt * P, (dt + 1) * P)
+            nc.vector.tensor_tensor(out=OT[c][:, :, cols], in0=zTs[i][:], in1=ST[c][:, :, cols], op=ALU.mult)
+            nc.vector.tensor_tensor(out=OT[c][:, :, cols], in0=qTs[i][:], in1=OT[c][:, :, cols], op=ALU.add)
+
+        sTs = {}
+        tqs = {}
+        oTs = {}
+
+        def xts(i):
+            c, dt = i // NDT, i % NDT
+            sT = pst.tile([P, 4, P], BF16, name="tp", tag="tp")
+            for jj in range(4):
+                nc.tensor.transpose(sT[:, jj, :], ST[c][:, jj, dt * P : (dt + 1) * P], identb[:])
+            sTs[i] = sT
+
+        def xvt(i):
+            tq = work.tile([P, 4, P], F32, name="tq", tag="tq", bufs=5)
+            nc.vector.tensor_tensor(
+                out=tq[:], in0=zs[i].rearrange("p (j r) -> p j r", j=4), in1=sTs[i][:], op=ALU.mult
+            )
+            tqs[i] = tq
+
+        def xtt(i):
+            oT = pst.tile([P, 4, P], F32, name="tp", tag="tp")
+            for jj in range(4):
+                nc.tensor.matmul(
+                    out=oT[:, jj, :], lhsT=tqs[i][:, jj, :], rhs=ident[:], is_transpose=True, start=True, stop=False
+                )
+                nc.tensor.matmul(
+                    out=oT[:, jj, :], lhsT=qs[i][:, jj * P : (jj + 1) * P], rhs=ident[:], is_transpose=True,
+                    start=False, stop=True,
+                )
+            oTs[i] = oT
+
+        def xev(i):
+            c, dt = i // NDT, i % NDT
+            if i >= VEVAC and i % 2 == 0:
+                nc.vector.tensor_copy(out=OT[c][:, :, dt * P : (dt + 1) * P], in_=oTs[i][:])
+            else:
+                nc.scalar.copy(out=OT[c][:, :, dt * P : (dt + 1) * P], in_=oTs[i][:])
+
+        def amax(c, jj, a, b, part):
+            col = (c * 4 + jj) * NPART + part
+            nc.vector.tensor_reduce(
+                out=am[:, col : col + 1], in_=OT[c][:, jj, a:b], axis=AX.X, op=ALU.max, apply_absolute_value=True
+            )
+
+        def fin(c):
+            sl = slice(4 * c, 4 * c + 4)
+            nc.vector.tensor_reduce(
+                out=fac[:, 0, sl],
+                in_=am[:, c * 4 * NPART : (c + 1) * 4 * NPART].rearrange("p (j n) -> p j n", n=NPART),
+                axis=AX.X,
+                op=ALU.max,
+            )
+            nc.vector.reciprocal(out=fac[:, 1, sl], in_=fac[:, 0, sl])
+            nc.vector.tensor_scalar(out=fac[:, 2, sl], in0=fac[:, 1, sl], scalar1=448.0, scalar2=None, op0=ALU.mult)
+
+        f8s = {}
+
+        def cast(c, jj, a, b, eng):
+            j = 4 * c + jj
+            if j not in f8s:
+                f8s[j] = work.tile([P, DH], FP8, name="f8", tag="f8", bufs=4)
+            r = fac[:, 2, j : j + 1]
+            if eng == "v":
+                nc.vector.tensor_scalar(
+                    out=f8s[j][:, a:b], in0=OT[c][:, jj, a:b], scalar1=r, scalar2=None, op0=ALU.mult, saturate=False
+                )
+            else:
+                nc.scalar.activation(
+                    out=f8s[j][:, a:b], in_=OT[c][:, jj, a:b], func=ACT.Identity, scale=r, bias=zero[:, 0:1],
+                    saturate=False,
+                )
+
+        def store1(c, jj):
+            j = 4 * c + jj
+            nc.sync.dma_start(out=o1_view[:, j, :], in_=f8s[j][:].bitcast(U8))
+
+        def store0(c, a, b):
+            cols = slice(a, b)
+            nc.sync.dma_start(out=o0_view[:, 4 * c : 4 * c + 4, cols], in_=OT[c][:, :, cols])
+
+        jwx = x_job("wx0", 0, rx0, [0], False)
+        piece(jwx, 0, "v")
+        piece(jwx, 1, "s")
+        bT = pst.tile([P, P], F32, name="tp", tag="tp")
+        nc.tensor.transpose(bT[:], brow32[:], ident[:])
+        nc.vector.tensor_copy(out=bias[:], in_=bT[:, 0 : 2 * NDT])
+        juh = x_job("uh0", 0, rx0, [1], False)
+        piece(juh, 0, "v")
+        piece(juh, 1, "s")
+        quant(jwx)
+        nc.vector.tensor_scalar(out=cst[:, 0:1], in0=sg[:, 0:1], scalar1=-1.0, scalar2=None, op0=ALU.mult)
+        nc.vector.tensor_tensor(out=cst[:, 1:2], in0=sg[:, 0:1], in1=sg[:, 1:2], op=ALU.add)
+        jw0 = w_job("w0", [0], False)
+        piece(jw0, 0, "s")
+        quant(juh)
+        quant(jw0)
+        jw1 = w_job("w1", [1], False)
+        piece(jw1, 0, "v")
+
+        def unit(i):
+            if i >= XFROM:
+                xts(i)
+            mx(i)
+            act(i)
+            if i >= XFROM:
+                xvt(i)
+            gq(i)
+
+        jw23 = w_job("w23", [2, 3], False)
+        piece(jw23, 0, "s")
+        quant(jw1)
+        piece(jw23, 1, "v")
+        for i in range(LOOK):
+            if i == 2:
+                quant(jw23)
+            unit(i)
+        rwg[3] = load_wg(3)
+        load_state(0, 3 * CH, 4 * CH)
+        jw45 = w_job("w45", [4, 5], False)
+        piece(jw45, 0, "s")
+        piece(jw45, 1, "v")
+        quant(jw45)
+        rx1 = []
+
+        jobs = {}
+        pieces_at = {0: [("w67", 0, "s"), ("w67", 1, "v")], 1: [("g2", 0, "s"), ("g2", 1, "v")],
+                     2: [("g2", 2, "s"), ("g2", 3, "v")]}
+        quant_at = {0: "w67", 2: "g2", 6: "g3", 10: "x1"}
+        for k in range(4):
+            pieces_at[3 + k] = [("g3", k, "s")]
+            pieces_at[7 + k] = [("x1", k, "s")]
+
+        def get_job(name):
+            if name not in jobs:
+                if name == "w67":
+                    jobs[name] = w_job(name, [6, 7], False)
+                elif name == "g2":
+                    jobs[name] = w_job(name, [8, 9, 10, 11], True)
+                elif name == "g3":
+                    jobs[name] = w_job(name, [12, 13, 14, 15], True)
+                else:
+                    jobs[name] = x_job(name, 1, rx1, [0, 1], True)
+            return jobs[name]
+
+        amax_at = {}
+        for jj in range(4):
+            amax_at[8 + jj] = [(0, jj, 0, 1024, 0)]
+            amax_at[16 + jj] = [(0, jj, 1024, 2048, 1)]
+            amax_at[20 + jj] = [(1, jj, 0, 512, 0)]
+            amax_at[24 + jj] = [(1, jj, 512, 1024, 4)]
+        amax_at[28] = [(1, 0, 1024, 1536, 1)]
+        amax_at[29] = [(1, 1, 1024, 1536, 1)]
+        amax_at[30] = [(1, 2, 1024, 1536, 1), (1, 3, 1024, 1536, 1)] + [(1, jj, 1536, 1920, 2) for jj in range(4)]
+        amax_at[31] = [(1, jj, 1920, 2048, 3) for jj in range(4)]
+
+        def last_started(s):
+            return min(NU - 1, s + (LOOK if s < LATE else LOOK_LATE))
+
+        for s in range(NU):
+            for i in range(last_started(s - 1) + 1, last_started(s) + 1):
+                unit(i)
+            if s >= XFROM:
+                xtt(s)
+                xev(s)
+            else:
+                tt(s)
+                vv(s)
+            if s % 4 == 3 and s != NU - 1:
+                store0(s // NDT, (s % NDT - 3) * P, (s % NDT + 1) * P)
+            if s in (NU - 3, NU - 1):
+                store0(1, (s % NDT - 1) * P, (s % NDT + 1) * P)
+            for name, k, eng in pieces_at.get(s, []):
+                piece(get_job(name), k, eng)
+            if s in quant_at:
+                quant(get_job(quant_at[s]))
+            if s == 1:
+                rx1.extend(load_x(1))
+                load_state(1, 0, 2 * CH)
+                load_state(1, 2 * CH, 4 * CH)
+            for c, jj, a, b, part in amax_at.get(s, []):
+                amax(c, jj, a, b, part)
+            if s == 19:
+                fin(0)
+            if CAST0 <= s < CAST0 + 8:
+                jj, h = (s - CAST0) // 2, (s - CAST0) % 2
+                cast(0, jj, h * 1024, (h + 1) * 1024, "s")
+                if h == 1:
+                    store1(0, jj)
+
+        fin(1)
+        for jj in range(4):
+            cast(1, jj, 0, VCAST, "v")
+            cast(1, jj, VCAST, DH, "s")
+            store1(1, jj)

@@ -21,15 +21,20 @@ NJ = 8
 NDT = 16
 CH = 512
 NU = 32
-LOOK = 3
-LOOK_LATE = 4
-LATE = 12
+NR = 8
 XFROM = 10
-BATCHES = [[i] for i in range(12)] + [[i, i + 1] for i in range(12, 30, 2)] + [[30], [31]]
+BATCHES = [[0], [1]] + [[i, i + 1] for i in range(2, 30, 2)] + [[30], [31]]
+LP = 2
+PA = 4
+QA = 3
+A0 = 8
 CAST0 = 23
 VEVAC = 20
+VMOD = 2
 NPART = 5
 VCAST = 1280
+WARM = 6
+PIECE_ENG = "ssv"
 
 
 def tile_fastgrnncudacell_pa_kernel(
@@ -38,7 +43,6 @@ def tile_fastgrnncudacell_pa_kernel(
     nc = tc.nc
     with ExitStack() as ctx:
         const = ctx.enter_context(tc.tile_pool(name="const", bufs=1))
-        rawp = ctx.enter_context(tc.tile_pool(name="rawp", bufs=6))
         keep = ctx.enter_context(tc.tile_pool(name="keep", bufs=1))
         grp = ctx.enter_context(tc.tile_pool(name="grp", bufs=2))
         work = ctx.enter_context(tc.tile_pool(name="work", bufs=4))
@@ -56,45 +60,48 @@ def tile_fastgrnncudacell_pa_kernel(
         nc.vector.memset(brow[:], 0.0)
         zt = const.tile([P, 1], BF16, name="zt", tag="zt")
         nt = const.tile([P, 1], BF16, name="nt", tag="nt")
-        nc.scalar.dma_start(out=zt[:], in_=zeta.to_broadcast([P, 1]))
-        nc.scalar.dma_start(out=nt[:], in_=nu.to_broadcast([P, 1]))
         nc.scalar.dma_start(out=brow[0:NDT, :], in_=bias_gate.rearrange("o (t m) -> (o t) m", m=P))
         nc.scalar.dma_start(out=brow[NDT : 2 * NDT, :], in_=bias_update.rearrange("o (t m) -> (o t) m", m=P))
+        nc.scalar.dma_start(out=zt[:], in_=zeta.to_broadcast([P, 1]))
+        nc.scalar.dma_start(out=nt[:], in_=nu.to_broadcast([P, 1]))
 
         ST = [keep.tile([P, 4, DH], BF16, name="st%d" % c, tag="st%d" % c) for c in range(2)]
-        OT = [keep.tile([P, 4, DH], F32, name="ot%d" % c, tag="ot%d" % c) for c in range(2)]
+        OT = [keep.tile([P, 4, DH], F32, name="ot0", tag="ot0")]
+        arena = keep.tile([P, 8, 4, RANK], BF16, name="arena", tag="arena", align_bytes=64)
+        ZR = keep.tile([P, NR, CH], F32, name="zr", tag="zr")
+        QR = keep.tile([P, NR, CH], F32, name="qr", tag="qr")
+        GT = keep.tile([P, 2, 2, CH], F32, name="gt", tag="gt")
+        TQ = keep.tile([P, 4, 4, P], F32, name="tq", tag="tq")
 
-        def load_x(c):
-            res = []
-            for op in range(2):
-                r = rawp.tile([P, 4, RANK], BF16, name="raw", tag="raw")
-                nc.sync.dma_start(out=r[:], in_=x_views[op][:, 4 * c : 4 * c + 4, :])
-                res.append(r)
-            return res
+        def load_x(c, slot, halves):
+            for h in halves:
+                for op in range(2):
+                    nc.sync.dma_start(
+                        out=arena[:, slot + op, 2 * h : 2 * h + 2, :], in_=x_views[op][:, 4 * c + 2 * h : 4 * c + 2 * h + 2, :]
+                    )
 
-        def load_wg(g):
-            res = []
+        def load_w1(dt):
             for op in range(2):
-                r = rawp.tile([P, 4, RANK], BF16, name="raw", tag="raw")
-                nc.sync.dma_start(out=r[:], in_=w_views[op][:, 4 * g : 4 * g + 4, :])
-                res.append(r)
-            return res
+                nc.sync.dma_start(out=arena[:, op, dt, :], in_=w_views[op][:, dt, :])
+
+        def load_wg(g, slot):
+            for op in range(2):
+                nc.sync.dma_start(out=arena[:, slot + op, :, :], in_=w_views[op][:, 4 * g : 4 * g + 4, :])
 
         def load_state(c, a, b):
             nc.sync.dma_start(out=ST[c][:, :, a:b], in_=st_view[:, 4 * c : 4 * c + 4, a:b])
 
-        rx0 = load_x(0)
-        rw0 = {}
-        for dt in range(4):
-            for op in range(2):
-                r = keep.tile([P, RANK], BF16, name="rw%d%d" % (dt, op), tag="rw%d%d" % (dt, op))
-                nc.sync.dma_start(out=r[:], in_=w_views[op][:, dt, :])
-                rw0[(dt, op)] = r
-        rwg = {}
-        rwg[1] = load_wg(1)
+        wslot = {0: 0, 1: 4, 2: 6, 3: 0}
+        xslot = {0: 2, 1: 2}
+        load_w1(0)
+        load_x(0, 2, [0, 1])
+        load_w1(1)
+        load_w1(2)
+        load_w1(3)
         load_state(0, 0, CH)
+        load_wg(1, 4)
         load_state(0, CH, 2 * CH)
-        rwg[2] = load_wg(2)
+        load_wg(2, 6)
         load_state(0, 2 * CH, 3 * CH)
 
         ident = const.tile([P, P], F32, name="ident", tag="ident")
@@ -107,24 +114,28 @@ def tile_fastgrnncudacell_pa_kernel(
         nc.vector.memset(am[:], 0.0)
         fac = const.tile([P, 3, 8], F32, name="fac", tag="fac")
         sg = const.tile([P, 2], F32, name="sg", tag="sg")
-        nc.scalar.activation(out=sg[:, 0:1], in_=zt[:], func=ACT.Sigmoid)
-        nc.scalar.activation(out=sg[:, 1:2], in_=nt[:], func=ACT.Sigmoid)
         cst = const.tile([P, 2], F32, name="cst", tag="cst")
         brow32 = const.tile([P, P], F32, name="brow32", tag="brow32")
-        nc.vector.tensor_copy(out=brow32[:], in_=brow[:])
         bias = const.tile([P, 2 * NDT], F32, name="bias", tag="bias")
+        nc.scalar.activation(out=sg[:, 0:1], in_=zero[:], func=ACT.Sigmoid)
+
+        if WARM:
+            wt = pst.tile([P, 4, P], F32, name="tp", tag="tp")
+            for n in range(WARM):
+                nc.tensor.matmul(out=wt[:, n % 4, :], lhsT=identb[:], rhs=identb[:], start=True, stop=True)
 
         wloc = {}
         xloc = {}
 
-        def new_job(name, srcs, big):
+        def new_job(name, srcs, big, codes=None, scales=None, off=0):
             n = len(srcs)
-            codes = keep.tile([P, n * P], U32, name="c" + name, tag="c" + name, align_bytes=64)
-            scales = keep.tile([P, n * P], U8, name="s" + name, tag="s" + name, align_bytes=64)
+            if codes is None:
+                codes = keep.tile([P, n * P], U32, name="c" + name, tag="c" + name, align_bytes=64)
+                scales = keep.tile([P, n * P], U8, name="s" + name, tag="s" + name, align_bytes=64)
             gtag = "grL" if big else "grS"
-            grouped = grp.tile([P, n * P * 4], BF16, name=gtag, tag=gtag, align_bytes=64, bufs=(1 if big else 2))
+            grouped = grp.tile([P, n * P * 4], BF16, name=gtag, tag=gtag, align_bytes=64, bufs=(1 if big else 3))
             g32 = grouped[:].bitcast(F32).rearrange("p (s r u) -> p s r u", s=n, u=2)
-            return {"srcs": srcs, "codes": codes, "scales": scales, "grouped": grouped, "g32": g32}
+            return {"srcs": srcs, "codes": codes, "scales": scales, "grouped": grouped, "g32": g32, "off": off, "n": n}
 
         def piece(job, k, eng):
             bank = pst.tile([P, 2, 2, P], F32, name="tp", tag="tp")
@@ -140,39 +151,37 @@ def tile_fastgrnncudacell_pa_kernel(
                 nc.scalar.copy(out=dst, in_=src)
 
         def quant(job):
+            a, n = job["off"], job["n"] * P
             nc.vector.quantize_mx(
-                out=job["codes"][:].bitcast(FP8X4), scales=job["scales"][:], in_=job["grouped"][:]
+                out=job["codes"][:, a : a + n].bitcast(FP8X4), scales=job["scales"][:, a : a + n], in_=job["grouped"][:]
             )
 
         def w_job(name, dts, big):
             srcs = []
             for dt in dts:
                 for op in range(2):
-                    if dt < 4:
-                        srcs.append(rw0[(dt, op)][:])
-                    else:
-                        srcs.append(rwg[dt // 4][op][:, dt % 4, :])
+                    srcs.append(arena[:, wslot[dt // 4] + op, dt % 4, :])
             job = new_job(name, srcs, big)
             for n, dt in enumerate(dts):
                 for op in range(2):
                     wloc[(dt, op)] = (job, (2 * n + op) * P)
             return job
 
-        def x_job(name, c, raws, ops, big):
-            srcs = []
-            for op in ops:
-                for jj in range(4):
-                    srcs.append(raws[op][:, jj, :])
-            job = new_job(name, srcs, big)
-            for n, op in enumerate(ops):
-                xloc[(c, op)] = (job, n * CH)
-            return job
-
         accs = {}
-        zs = {}
-        qs = {}
         zTs = {}
         qTs = {}
+        batch_of = {}
+        bidx = {}
+        for n, units in enumerate(BATCHES):
+            for i in units:
+                batch_of[i] = units
+                bidx[i] = n
+
+        def zs(i):
+            return ZR[:, i % NR, :]
+
+        def qs(i):
+            return QR[:, i % NR, :]
 
         def mx(i):
             c, dt = i // NDT, i % NDT
@@ -184,52 +193,38 @@ def tile_fastgrnncudacell_pa_kernel(
                     out=acc[:],
                     lhsT=wj["codes"][:, wo : wo + P].bitcast(FP8X4),
                     lhsT_scale=wj["scales"][:, wo : wo + P],
-                    rhs=xj["codes"][:, xo : xo + CH].bitcast(FP8X4),
-                    rhs_scale=xj["scales"][:, xo : xo + CH],
+                    rhs=xj[0][:, xo : xo + CH].bitcast(FP8X4),
+                    rhs_scale=xj[1][:, xo : xo + CH],
                     start=(op == 0),
                     stop=(op == 1),
                 )
             accs[i] = acc
 
-        batch_of = {}
-        for units in BATCHES:
-            for i in units:
-                batch_of[i] = units
-        zb = {}
-        qb = {}
-
         def act(i):
             dt = i % NDT
-            units = batch_of[i]
-            if i == units[0]:
-                zb[i] = work.tile([P, len(units), CH], F32, name="z", tag="z")
-                qb[i] = work.tile([P, len(units), CH], F32, name="q", tag="q")
-            k = i - units[0]
-            zs[i] = zb[units[0]][:, k, :]
-            qs[i] = qb[units[0]][:, k, :]
-            nc.scalar.activation(out=zs[i], in_=accs[i][:], func=ACT.Sigmoid, bias=bias[:, dt : dt + 1], scale=1.0)
+            nc.scalar.activation(out=zs(i), in_=accs[i][:], func=ACT.Sigmoid, bias=bias[:, dt : dt + 1], scale=1.0)
             nc.scalar.activation(
-                out=qs[i], in_=accs[i][:], func=ACT.Tanh, bias=bias[:, NDT + dt : NDT + dt + 1], scale=1.0
+                out=qs(i), in_=accs[i][:], func=ACT.Tanh, bias=bias[:, NDT + dt : NDT + dt + 1], scale=1.0
             )
 
         def gq(i):
             units = batch_of[i]
             if i != units[-1]:
                 return
-            z, q = zb[units[0]], qb[units[0]]
-            gt = work.tile([P, len(units), CH], F32, name="gt", tag="gt", bufs=2)
+            a, n = units[0] % NR, len(units)
+            g = GT[:, bidx[i] % 2, 0:n, :]
             nc.gpsimd.tensor_scalar(
-                out=gt[:], in0=z[:], scalar1=cst[:, 0:1], scalar2=cst[:, 1:2], op0=ALU.mult, op1=ALU.add
+                out=g, in0=ZR[:, a : a + n, :], scalar1=cst[:, 0:1], scalar2=cst[:, 1:2], op0=ALU.mult, op1=ALU.add
             )
-            nc.gpsimd.tensor_tensor(out=q[:], in0=gt[:], in1=q[:], op=ALU.mult)
+            nc.gpsimd.tensor_tensor(out=QR[:, a : a + n, :], in0=g, in1=QR[:, a : a + n, :], op=ALU.mult)
 
         def tt(i):
             zT = pst.tile([P, 4, P], F32, name="tp", tag="tp")
             qT = pst.tile([P, 4, P], F32, name="tp", tag="tp")
             for jj in range(4):
-                nc.tensor.transpose(zT[:, jj, :], zs[i][:, jj * P : (jj + 1) * P], ident[:])
+                nc.tensor.transpose(zT[:, jj, :], zs(i)[:, jj * P : (jj + 1) * P], ident[:])
             for jj in range(4):
-                nc.tensor.transpose(qT[:, jj, :], qs[i][:, jj * P : (jj + 1) * P], ident[:])
+                nc.tensor.transpose(qT[:, jj, :], qs(i)[:, jj * P : (jj + 1) * P], ident[:])
             zTs[i] = zT
             qTs[i] = qT
 
@@ -240,7 +235,6 @@ def tile_fastgrnncudacell_pa_kernel(
             nc.vector.tensor_tensor(out=OT[c][:, :, cols], in0=qTs[i][:], in1=OT[c][:, :, cols], op=ALU.add)
 
         sTs = {}
-        tqs = {}
         oTs = {}
 
         def xts(i):
@@ -251,27 +245,25 @@ def tile_fastgrnncudacell_pa_kernel(
             sTs[i] = sT
 
         def xvt(i):
-            tq = work.tile([P, 4, P], F32, name="tq", tag="tq", bufs=5)
             nc.vector.tensor_tensor(
-                out=tq[:], in0=zs[i].rearrange("p (j r) -> p j r", j=4), in1=sTs[i][:], op=ALU.mult
+                out=TQ[:, i % 4], in0=zs(i).rearrange("p (j r) -> p j r", j=4), in1=sTs[i][:], op=ALU.mult
             )
-            tqs[i] = tq
 
         def xtt(i):
             oT = pst.tile([P, 4, P], F32, name="tp", tag="tp")
             for jj in range(4):
                 nc.tensor.matmul(
-                    out=oT[:, jj, :], lhsT=tqs[i][:, jj, :], rhs=ident[:], is_transpose=True, start=True, stop=False
+                    out=oT[:, jj, :], lhsT=TQ[:, i % 4, jj, :], rhs=ident[:], is_transpose=True, start=True, stop=False
                 )
                 nc.tensor.matmul(
-                    out=oT[:, jj, :], lhsT=qs[i][:, jj * P : (jj + 1) * P], rhs=ident[:], is_transpose=True,
+                    out=oT[:, jj, :], lhsT=qs(i)[:, jj * P : (jj + 1) * P], rhs=ident[:], is_transpose=True,
                     start=False, stop=True,
                 )
             oTs[i] = oT
 
         def xev(i):
             c, dt = i // NDT, i % NDT
-            if i >= VEVAC and i % 2 == 0:
+            if i >= VEVAC and i % VMOD == 0:
                 nc.vector.tensor_copy(out=OT[c][:, :, dt * P : (dt + 1) * P], in_=oTs[i][:])
             else:
                 nc.scalar.copy(out=OT[c][:, :, dt * P : (dt + 1) * P], in_=oTs[i][:])
@@ -318,73 +310,77 @@ def tile_fastgrnncudacell_pa_kernel(
             cols = slice(a, b)
             nc.sync.dma_start(out=o0_view[:, 4 * c : 4 * c + 4, cols], in_=OT[c][:, :, cols])
 
-        jwx = x_job("wx0", 0, rx0, [0], False)
-        piece(jwx, 0, "v")
-        piece(jwx, 1, "s")
-        bT = pst.tile([P, P], F32, name="tp", tag="tp")
-        nc.tensor.transpose(bT[:], brow32[:], ident[:])
-        nc.vector.tensor_copy(out=bias[:], in_=bT[:, 0 : 2 * NDT])
-        juh = x_job("uh0", 0, rx0, [1], False)
-        piece(juh, 0, "v")
-        piece(juh, 1, "s")
-        quant(jwx)
-        nc.vector.tensor_scalar(out=cst[:, 0:1], in0=sg[:, 0:1], scalar1=-1.0, scalar2=None, op0=ALU.mult)
-        nc.vector.tensor_tensor(out=cst[:, 1:2], in0=sg[:, 0:1], in1=sg[:, 1:2], op=ALU.add)
+        xc = [keep.tile([P, 2 * CH], U32, name="xc%d" % c, tag="xc%d" % c, align_bytes=64) for c in range(2)]
+        xs = [keep.tile([P, 2 * CH], U8, name="xs%d" % c, tag="xs%d" % c, align_bytes=64) for c in range(2)]
+        for c in range(2):
+            for op in range(2):
+                xloc[(c, op)] = ((xc[c], xs[c]), op * CH)
+
+        def x_half(c, op, h):
+            srcs = [arena[:, xslot[c] + op, 2 * h + r, :] for r in range(2)]
+            return new_job("x", srcs, False, xc[c], xs[c], op * CH + h * 2 * P)
+
         jw0 = w_job("w0", [0], False)
         piece(jw0, 0, "s")
-        quant(juh)
+        ja = x_half(0, 0, 0)
+        piece(ja, 0, "v")
+        jb = x_half(0, 1, 0)
+        piece(jb, 0, "s")
         quant(jw0)
-        jw1 = w_job("w1", [1], False)
-        piece(jw1, 0, "v")
-
-        def unit(i):
-            if i >= XFROM:
-                xts(i)
-            mx(i)
-            act(i)
-            if i >= XFROM:
-                xvt(i)
-            gq(i)
-
-        jw23 = w_job("w23", [2, 3], False)
-        piece(jw23, 0, "s")
-        quant(jw1)
-        piece(jw23, 1, "v")
-        for i in range(LOOK):
-            if i == 2:
-                quant(jw23)
-            unit(i)
-        rwg[3] = load_wg(3)
-        load_state(0, 3 * CH, 4 * CH)
-        jw45 = w_job("w45", [4, 5], False)
-        piece(jw45, 0, "s")
-        piece(jw45, 1, "v")
-        quant(jw45)
-        rx1 = []
+        jc = x_half(0, 0, 1)
+        piece(jc, 0, "v")
+        quant(ja)
+        nc.vector.tensor_copy(out=brow32[:], in_=brow[:])
+        jd = x_half(0, 1, 1)
+        piece(jd, 0, "s")
+        quant(jb)
+        bT = pst.tile([P, P], F32, name="tp", tag="tp")
+        nc.tensor.transpose(bT[:], brow32[:], ident[:])
+        quant(jc)
+        nc.vector.tensor_copy(out=bias[:], in_=bT[:, 0 : 2 * NDT])
+        quant(jd)
+        nc.scalar.activation(out=sg[:, 0:1], in_=zt[:], func=ACT.Sigmoid)
+        nc.scalar.activation(out=sg[:, 1:2], in_=nt[:], func=ACT.Sigmoid)
+        nc.vector.tensor_scalar(out=cst[:, 0:1], in0=sg[:, 0:1], scalar1=-1.0, scalar2=None, op0=ALU.mult)
+        nc.vector.tensor_tensor(out=cst[:, 1:2], in0=sg[:, 0:1], in1=sg[:, 1:2], op=ALU.add)
 
         jobs = {}
-        pieces_at = {0: [("w67", 0, "s"), ("w67", 1, "v")], 1: [("g2", 0, "s"), ("g2", 1, "v")],
-                     2: [("g2", 2, "s"), ("g2", 3, "v")]}
-        quant_at = {0: "w67", 2: "g2", 6: "g3", 10: "x1"}
-        for k in range(4):
-            pieces_at[3 + k] = [("g3", k, "s")]
-            pieces_at[7 + k] = [("x1", k, "s")]
 
         def get_job(name):
             if name not in jobs:
-                if name == "w67":
-                    jobs[name] = w_job(name, [6, 7], False)
-                elif name == "g2":
-                    jobs[name] = w_job(name, [8, 9, 10, 11], True)
-                elif name == "g3":
-                    jobs[name] = w_job(name, [12, 13, 14, 15], True)
+                if name[0] == "w":
+                    p = int(name[1:])
+                    jobs[name] = w_job("p" + name, [1] if p == 0 else [2 * p, 2 * p + 1], False)
                 else:
-                    jobs[name] = x_job(name, 1, rx1, [0, 1], True)
+                    op = int(name[1:])
+                    srcs = [arena[:, xslot[1] + op, r, :] for r in range(4)]
+                    jobs[name] = new_job("x", srcs, False, xc[1], xs[1], op * CH)
             return jobs[name]
+
+        order = ["w%d" % p for p in range(0, 8)] + ["x0", "x1"]
+        pieces_done = [0]
+        quants_done = [0]
+
+        def prep_pieces(n):
+            while pieces_done[0] < min(n, len(order)):
+                j = get_job(order[pieces_done[0]])
+                for kk in range(len(j["srcs"]) // 2):
+                    piece(j, kk, PIECE_ENG[(2 * pieces_done[0] + kk) % len(PIECE_ENG)])
+                pieces_done[0] += 1
+
+        def prep_quants(n):
+            while quants_done[0] < min(n, pieces_done[0]):
+                quant(get_job(order[quants_done[0]]))
+                quants_done[0] += 1
+
+        def front(i):
+            mx(i)
+            act(i)
+            gq(i)
 
         amax_at = {}
         for jj in range(4):
-            amax_at[8 + jj] = [(0, jj, 0, 1024, 0)]
+            amax_at[A0 + jj] = [(0, jj, 0, 1024, 0)]
             amax_at[16 + jj] = [(0, jj, 1024, 2048, 1)]
             amax_at[20 + jj] = [(1, jj, 0, 512, 0)]
             amax_at[24 + jj] = [(1, jj, 512, 1024, 4)]
@@ -393,30 +389,11 @@ def tile_fastgrnncudacell_pa_kernel(
         amax_at[30] = [(1, 2, 1024, 1536, 1), (1, 3, 1024, 1536, 1)] + [(1, jj, 1536, 1920, 2) for jj in range(4)]
         amax_at[31] = [(1, jj, 1920, 2048, 3) for jj in range(4)]
 
-        def last_started(s):
-            return min(NU - 1, s + (LOOK if s < LATE else LOOK_LATE))
-
-        for s in range(NU):
-            for i in range(last_started(s - 1) + 1, last_started(s) + 1):
-                unit(i)
-            if s >= XFROM:
-                xtt(s)
-                xev(s)
-            else:
-                tt(s)
-                vv(s)
+        def after(s):
             if s % 4 == 3 and s != NU - 1:
                 store0(s // NDT, (s % NDT - 3) * P, (s % NDT + 1) * P)
             if s in (NU - 3, NU - 1):
                 store0(1, (s % NDT - 1) * P, (s % NDT + 1) * P)
-            for name, k, eng in pieces_at.get(s, []):
-                piece(get_job(name), k, eng)
-            if s in quant_at:
-                quant(get_job(quant_at[s]))
-            if s == 1:
-                rx1.extend(load_x(1))
-                load_state(1, 0, 2 * CH)
-                load_state(1, 2 * CH, 4 * CH)
             for c, jj, a, b, part in amax_at.get(s, []):
                 amax(c, jj, a, b, part)
             if s == 19:
@@ -426,6 +403,49 @@ def tile_fastgrnncudacell_pa_kernel(
                 cast(0, jj, h * 1024, (h + 1) * 1024, "s")
                 if h == 1:
                     store1(0, jj)
+
+        prep_pieces(1)
+        prep_quants(1)
+        for kp in range(-LP, NU // 2):
+            f = kp + LP
+            if f < NU // 2:
+                prep_quants(f + QA)
+                mx(2 * f)
+                mx(2 * f + 1)
+                act(2 * f)
+                gq(2 * f)
+                act(2 * f + 1)
+                gq(2 * f + 1)
+            if f == 1:
+                load_wg(3, 0)
+                load_state(0, 3 * CH, 4 * CH)
+            if f == 2:
+                load_x(1, 2, [0, 1])
+                load_state(1, 0, 2 * CH)
+                load_state(1, 2 * CH, 4 * CH)
+            md = kp + 1
+            if 0 <= md < NU // 2 and 2 * md >= XFROM:
+                xts(2 * md)
+                xts(2 * md + 1)
+                xvt(2 * md)
+                xvt(2 * md + 1)
+            if kp >= 0:
+                if 2 * kp == NDT:
+                    OT.append(keep.tile([P, 4, DH], F32, name="arena", tag="arena", align_bytes=64))
+                for s in (2 * kp, 2 * kp + 1):
+                    if s >= XFROM:
+                        xtt(s)
+                    else:
+                        tt(s)
+                for s in (2 * kp, 2 * kp + 1):
+                    if s >= XFROM:
+                        xev(s)
+                    else:
+                        vv(s)
+            prep_pieces(f + PA)
+            if kp >= 0:
+                after(2 * kp)
+                after(2 * kp + 1)
 
         fin(1)
         for jj in range(4):

@@ -25,15 +25,21 @@ NR = 8
 XFROM = 10
 BATCHES = [[0], [1]] + [[i, i + 1] for i in range(2, 30, 2)] + [[30], [31]]
 LP = 2
-PA = 4
-QA = 3
+PA = 5
+P0 = 2
+QV = ()
+GRSB = 3
+PR = 2
+QA = 4
 A0 = 8
 CAST0 = 23
 VEVAC = 20
 VMOD = 2
+VEND = 32
 NPART = 5
 VCAST = 1280
 WARM = 6
+C0ENG = "s"
 PIECE_ENG = "ssv"
 
 
@@ -133,7 +139,7 @@ def tile_fastgrnncudacell_pa_kernel(
                 codes = keep.tile([P, n * P], U32, name="c" + name, tag="c" + name, align_bytes=64)
                 scales = keep.tile([P, n * P], U8, name="s" + name, tag="s" + name, align_bytes=64)
             gtag = "grL" if big else "grS"
-            grouped = grp.tile([P, n * P * 4], BF16, name=gtag, tag=gtag, align_bytes=64, bufs=(1 if big else 3))
+            grouped = grp.tile([P, n * P * 4], BF16, name=gtag, tag=gtag, align_bytes=64, bufs=(1 if big else GRSB))
             g32 = grouped[:].bitcast(F32).rearrange("p (s r u) -> p s r u", s=n, u=2)
             return {"srcs": srcs, "codes": codes, "scales": scales, "grouped": grouped, "g32": g32, "off": off, "n": n}
 
@@ -207,16 +213,17 @@ def tile_fastgrnncudacell_pa_kernel(
                 out=qs(i), in_=accs[i][:], func=ACT.Tanh, bias=bias[:, NDT + dt : NDT + dt + 1], scale=1.0
             )
 
-        def gq(i):
+        def gq(i, late=False):
             units = batch_of[i]
-            if i != units[-1]:
+            if i != units[-1] or (i in QV) != late:
                 return
             a, n = units[0] % NR, len(units)
             g = GT[:, bidx[i] % 2, 0:n, :]
-            nc.gpsimd.tensor_scalar(
+            eng = nc.vector if i in QV else nc.gpsimd
+            eng.tensor_scalar(
                 out=g, in0=ZR[:, a : a + n, :], scalar1=cst[:, 0:1], scalar2=cst[:, 1:2], op0=ALU.mult, op1=ALU.add
             )
-            nc.gpsimd.tensor_tensor(out=QR[:, a : a + n, :], in0=g, in1=QR[:, a : a + n, :], op=ALU.mult)
+            eng.tensor_tensor(out=QR[:, a : a + n, :], in0=g, in1=QR[:, a : a + n, :], op=ALU.mult)
 
         def tt(i):
             zT = pst.tile([P, 4, P], F32, name="tp", tag="tp")
@@ -263,7 +270,7 @@ def tile_fastgrnncudacell_pa_kernel(
 
         def xev(i):
             c, dt = i // NDT, i % NDT
-            if i >= VEVAC and i % VMOD == 0:
+            if VEVAC <= i < VEND and i % VMOD == 0:
                 nc.vector.tensor_copy(out=OT[c][:, :, dt * P : (dt + 1) * P], in_=oTs[i][:])
             else:
                 nc.scalar.copy(out=OT[c][:, :, dt * P : (dt + 1) * P], in_=oTs[i][:])
@@ -400,11 +407,11 @@ def tile_fastgrnncudacell_pa_kernel(
                 fin(0)
             if CAST0 <= s < CAST0 + 8:
                 jj, h = (s - CAST0) // 2, (s - CAST0) % 2
-                cast(0, jj, h * 1024, (h + 1) * 1024, "s")
+                cast(0, jj, h * 1024, (h + 1) * 1024, C0ENG[(s - CAST0) % len(C0ENG)])
                 if h == 1:
                     store1(0, jj)
 
-        prep_pieces(1)
+        prep_pieces(P0)
         prep_quants(1)
         for kp in range(-LP, NU // 2):
             f = kp + LP
@@ -429,6 +436,8 @@ def tile_fastgrnncudacell_pa_kernel(
                 xts(2 * md + 1)
                 xvt(2 * md)
                 xvt(2 * md + 1)
+                gq(2 * md, True)
+                gq(2 * md + 1, True)
             if kp >= 0:
                 if 2 * kp == NDT:
                     OT.append(keep.tile([P, 4, DH], F32, name="arena", tag="arena", align_bytes=64))
@@ -442,7 +451,7 @@ def tile_fastgrnncudacell_pa_kernel(
                         xev(s)
                     else:
                         vv(s)
-            prep_pieces(f + PA)
+            prep_pieces(min(f + PA, P0 + 1 + PR * f))
             if kp >= 0:
                 after(2 * kp)
                 after(2 * kp + 1)

@@ -27,13 +27,16 @@ BATCHES = [[0], [1]] + [[i, i + 1] for i in range(2, 30, 2)] + [[30], [31]]
 LP = 2
 PA = 5
 P0 = 2
+LORD = 0
+TSRC = "gggs"
+NG = 4
 QV = ()
 GRSB = 3
 PR = 2
 QA = 4
 A0 = 8
 CAST0 = 23
-VEVAC = 20
+VEVAC = 12
 VMOD = 2
 VEND = 32
 NPART = 5
@@ -76,7 +79,7 @@ def tile_fastgrnncudacell_pa_kernel(
         arena = keep.tile([P, 8, 4, RANK], BF16, name="arena", tag="arena", align_bytes=64)
         ZR = keep.tile([P, NR, CH], F32, name="zr", tag="zr")
         QR = keep.tile([P, NR, CH], F32, name="qr", tag="qr")
-        GT = keep.tile([P, 2, 2, CH], F32, name="gt", tag="gt")
+        GT = keep.tile([P, NG, 2, CH], F32, name="gt", tag="gt")
         TQ = keep.tile([P, 4, 4, P], F32, name="tq", tag="tq")
 
         def load_x(c, slot, halves):
@@ -104,11 +107,23 @@ def tile_fastgrnncudacell_pa_kernel(
         load_w1(1)
         load_w1(2)
         load_w1(3)
-        load_state(0, 0, CH)
-        load_wg(1, 4)
-        load_state(0, CH, 2 * CH)
-        load_wg(2, 6)
-        load_state(0, 2 * CH, 3 * CH)
+        if LORD == 0:
+            load_state(0, 0, CH)
+            load_wg(1, 4)
+            load_state(0, CH, 2 * CH)
+            load_wg(2, 6)
+            load_state(0, 2 * CH, 3 * CH)
+        elif LORD == 1:
+            load_wg(1, 4)
+            load_state(0, 0, CH)
+            load_wg(2, 6)
+            load_state(0, CH, 2 * CH)
+            load_state(0, 2 * CH, 3 * CH)
+        else:
+            load_wg(1, 4)
+            load_wg(2, 6)
+            load_state(0, 0, 2 * CH)
+            load_state(0, 2 * CH, 3 * CH)
 
         ident = const.tile([P, P], F32, name="ident", tag="ident")
         make_identity(nc, ident[:])
@@ -212,18 +227,37 @@ def tile_fastgrnncudacell_pa_kernel(
             nc.scalar.activation(
                 out=qs(i), in_=accs[i][:], func=ACT.Tanh, bias=bias[:, NDT + dt : NDT + dt + 1], scale=1.0
             )
+            if tsrc(i) == "s":
+                nc.scalar.activation(
+                    out=GT[:, bidx[i] % NG, batch_of[i].index(i), :], in_=zs(i), func=ACT.Identity,
+                    scale=cst[:, 0:1], bias=cst[:, 1:2],
+                )
+
+        def tsrc(i):
+            return TSRC[bidx[i] % len(TSRC)]
+
+        pend = []
 
         def gq(i, late=False):
             units = batch_of[i]
-            if i != units[-1] or (i in QV) != late:
+            if i != units[-1]:
+                return
+            if (tsrc(i) == "v" or i in QV) and not late:
+                pend.append(i)
                 return
             a, n = units[0] % NR, len(units)
-            g = GT[:, bidx[i] % 2, 0:n, :]
-            eng = nc.vector if i in QV else nc.gpsimd
-            eng.tensor_scalar(
-                out=g, in0=ZR[:, a : a + n, :], scalar1=cst[:, 0:1], scalar2=cst[:, 1:2], op0=ALU.mult, op1=ALU.add
-            )
-            eng.tensor_tensor(out=QR[:, a : a + n, :], in0=g, in1=QR[:, a : a + n, :], op=ALU.mult)
+            g = GT[:, bidx[i] % NG, 0:n, :]
+            if tsrc(i) != "s":
+                eng = nc.vector if (tsrc(i) == "v" or i in QV) else nc.gpsimd
+                eng.tensor_scalar(
+                    out=g, in0=ZR[:, a : a + n, :], scalar1=cst[:, 0:1], scalar2=cst[:, 1:2], op0=ALU.mult, op1=ALU.add
+                )
+            eng2 = nc.vector if i in QV else nc.gpsimd
+            eng2.tensor_tensor(out=QR[:, a : a + n, :], in0=g, in1=QR[:, a : a + n, :], op=ALU.mult)
+
+        def flush():
+            while pend:
+                gq(pend.pop(0), True)
 
         def tt(i):
             zT = pst.tile([P, 4, P], F32, name="tp", tag="tp")
@@ -417,6 +451,7 @@ def tile_fastgrnncudacell_pa_kernel(
             f = kp + LP
             if f < NU // 2:
                 prep_quants(f + QA)
+                flush()
                 mx(2 * f)
                 mx(2 * f + 1)
                 act(2 * f)
@@ -430,14 +465,14 @@ def tile_fastgrnncudacell_pa_kernel(
                 load_x(1, 2, [0, 1])
                 load_state(1, 0, 2 * CH)
                 load_state(1, 2 * CH, 4 * CH)
+            if f >= NU // 2:
+                flush()
             md = kp + 1
             if 0 <= md < NU // 2 and 2 * md >= XFROM:
                 xts(2 * md)
                 xts(2 * md + 1)
                 xvt(2 * md)
                 xvt(2 * md + 1)
-                gq(2 * md, True)
-                gq(2 * md + 1, True)
             if kp >= 0:
                 if 2 * kp == NDT:
                     OT.append(keep.tile([P, 4, DH], F32, name="arena", tag="arena", align_bytes=64))

@@ -21,10 +21,13 @@ NJ = 8
 NDT = 16
 CH = 512
 NU = 32
-NR = 8
+NR = 12
 XFROM = 10
 BATCHES = [[0], [1]] + [[i, i + 1] for i in range(2, 30, 2)] + [[30], [31]]
 LP = 2
+LP2 = 3
+NPSA = 3
+KL = 10
 PA = 5
 P0 = 2
 LORD = 0
@@ -55,8 +58,8 @@ def tile_fastgrnncudacell_pa_kernel(
         keep = ctx.enter_context(tc.tile_pool(name="keep", bufs=1))
         grp = ctx.enter_context(tc.tile_pool(name="grp", bufs=2))
         work = ctx.enter_context(tc.tile_pool(name="work", bufs=4))
-        psa = ctx.enter_context(tc.psum_pool(name="psa", bufs=2))
-        pst = ctx.enter_context(tc.psum_pool(name="pst", bufs=6))
+        psa = ctx.enter_context(tc.psum_pool(name="psa", bufs=NPSA))
+        pst = ctx.enter_context(tc.psum_pool(name="pst", bufs=8 - NPSA))
         ctx.enter_context(tc.manual_schedule())
 
         x_views = [a.rearrange("(p j) k -> p j k", j=NJ) for a in (wx_r, uh_r)]
@@ -447,9 +450,12 @@ def tile_fastgrnncudacell_pa_kernel(
 
         prep_pieces(P0)
         prep_quants(1)
+        fnext = [0]
         for kp in range(-LP, NU // 2):
-            f = kp + LP
-            if f < NU // 2:
+            target = kp + (LP if kp < KL else LP2)
+            f = fnext[0]
+            while fnext[0] <= min(target, NU // 2 - 1):
+                f = fnext[0]
                 prep_quants(f + QA)
                 flush()
                 mx(2 * f)
@@ -458,14 +464,15 @@ def tile_fastgrnncudacell_pa_kernel(
                 gq(2 * f)
                 act(2 * f + 1)
                 gq(2 * f + 1)
-            if f == 1:
-                load_wg(3, 0)
-                load_state(0, 3 * CH, 4 * CH)
-            if f == 2:
-                load_x(1, 2, [0, 1])
-                load_state(1, 0, 2 * CH)
-                load_state(1, 2 * CH, 4 * CH)
-            if f >= NU // 2:
+                if f == 1:
+                    load_wg(3, 0)
+                    load_state(0, 3 * CH, 4 * CH)
+                if f == 2:
+                    load_x(1, 2, [0, 1])
+                    load_state(1, 0, 2 * CH)
+                    load_state(1, 2 * CH, 4 * CH)
+                fnext[0] += 1
+            if fnext[0] >= NU // 2:
                 flush()
             md = kp + 1
             if 0 <= md < NU // 2 and 2 * md >= XFROM:

@@ -111,11 +111,9 @@ def tile_fastgrnncudacell_pa_kernel(
         load_w1(2)
         load_w1(3)
         if LORD == 0:
-            load_state(0, 0, CH)
             load_wg(1, 4)
-            load_state(0, CH, 2 * CH)
+            load_state(0, 0, 2 * CH)
             load_wg(2, 6)
-            load_state(0, 2 * CH, 3 * CH)
         elif LORD == 1:
             load_wg(1, 4)
             load_state(0, 0, CH)
@@ -434,8 +432,10 @@ def tile_fastgrnncudacell_pa_kernel(
         amax_at[31] = [(1, jj, 1920, 2048, 3) for jj in range(4)]
 
         def after(s):
-            if s % 4 == 3 and s != NU - 1:
-                store0(s // NDT, (s % NDT - 3) * P, (s % NDT + 1) * P)
+            if s % 8 == 7 and s != NU - 1:
+                store0(s // NDT, (s % NDT - 7) * P, (s % NDT + 1) * P)
+            if s == NU - 5:
+                store0(1, (s % NDT - 3) * P, (s % NDT + 1) * P)
             if s in (NU - 3, NU - 1):
                 store0(1, (s % NDT - 1) * P, (s % NDT + 1) * P)
             for c, jj, a, b, part in amax_at.get(s, []):
@@ -466,7 +466,7 @@ def tile_fastgrnncudacell_pa_kernel(
                 gq(2 * f + 1)
                 if f == 1:
                     load_wg(3, 0)
-                    load_state(0, 3 * CH, 4 * CH)
+                    load_state(0, 2 * CH, 4 * CH)
                 if f == 2:
                     load_x(1, 2, [0, 1])
                     load_state(1, 0, 2 * CH)

@@ -37,13 +37,13 @@ QV = ()
 GRSB = 3
 PR = 2
 QA = 4
-A0 = 8
-CAST0 = 23
+A0 = 10
+CAST0 = 24
 VEVAC = 12
 VMOD = 2
 VEND = 32
 NPART = 5
-VCAST = 1280
+VCAST = 1408
 WARM = 6
 C0ENG = "s"
 PIECE_ENG = "ssv"

@@ -332,7 +332,7 @@ def tile_fastgrnncudacell_pa_kernel(
         def cast(c, jj, a, b, eng):
             j = 4 * c + jj
             if j not in f8s:
-                f8s[j] = work.tile([P, DH], FP8, name="f8", tag="f8", bufs=4)
+                f8s[j] = work.tile([P, DH], FP8, name="f8", tag="f8", bufs=6)
             r = fac[:, 2, j : j + 1]
             if eng == "v":
                 nc.vector.tensor_scalar(

from contextlib import ExitStack

import concourse.mybir as mybir
from concourse.masks import make_identity

B, DH, RANK = 1024, 2048, 512
FLOPS = 2 * B * DH * 2 * RANK

F32 = mybir.dt.float32
BF16 = mybir.dt.bfloat16
U32 = mybir.dt.uint32
U8 = mybir.dt.uint8
FP8X4 = mybir.dt.float8_e4m3fn_x4
FP8 = mybir.dt.float8_e4m3fn
ACT = mybir.ActivationFunctionType
ALU = mybir.AluOpType
AX = mybir.AxisListType

P = 128
NJ = 8
NDT = 16
CH = 512
NU = 32
NR = 12
XFROM = 10
BATCHES = [[0], [1]] + [[i, i + 1] for i in range(2, 30, 2)] + [[30], [31]]
LP = 2
LP2 = 3
NPSA = 3
KL = 10
PA = 5
P0 = 2
LORD = 0
TSRC = "gggs"
NG = 4
QV = ()
GRSB = 3
PR = 2
QA = 4
A0 = 10
CAST0 = 24
VEVAC = 12
VMOD = 2
VEND = 32
NPART = 5
VCAST = 1408
WARM = 6
C0ENG = "s"
PIECE_ENG = "ssv"


def tile_fastgrnncudacell_pa_kernel(
    tc, wx_r, uh_r, state, W2, U2, bias_gate, bias_update, zeta, nu, out_0, out_1
):
    nc = tc.nc
    with ExitStack() as ctx:
        const = ctx.enter_context(tc.tile_pool(name="const", bufs=1))
        keep = ctx.enter_context(tc.tile_pool(name="keep", bufs=1))
        grp = ctx.enter_context(tc.tile_pool(name="grp", bufs=2))
        work = ctx.enter_context(tc.tile_pool(name="work", bufs=4))
        psa = ctx.enter_context(tc.psum_pool(name="psa", bufs=NPSA))
        pst = ctx.enter_context(tc.psum_pool(name="pst", bufs=8 - NPSA))
        ctx.enter_context(tc.manual_schedule())

        x_views = [a.rearrange("(p j) k -> p j k", j=NJ) for a in (wx_r, uh_r)]
        w_views = [a.rearrange("(t m) k -> m t k", m=P) for a in (W2, U2)]
        st_view = state.rearrange("(p j) d -> p j d", j=NJ)
        o0_view = out_0.rearrange("(p j) d -> p j d", j=NJ)
        o1_view = out_1.rearrange("(p j) d -> p j d", j=NJ)

        brow = const.tile([P, P], BF16, name="brow", tag="brow")
        nc.vector.memset(brow[:], 0.0)
        zt = const.tile([P, 1], BF16, name="zt", tag="zt")
        nt = const.tile([P, 1], BF16, name="nt", tag="nt")
        nc.scalar.dma_start(out=brow[0:NDT, :], in_=bias_gate.rearrange("o (t m) -> (o t) m", m=P))
        nc.scalar.dma_start(out=brow[NDT : 2 * NDT, :], in_=bias_update.rearrange("o (t m) -> (o t) m", m=P))
        nc.scalar.dma_start(out=zt[:], in_=zeta.to_broadcast([P, 1]))
        nc.scalar.dma_start(out=nt[:], in_=nu.to_broadcast([P, 1]))

        ST = [keep.tile([P, 4, DH], BF16, name="st%d" % c, tag="st%d" % c) for c in range(2)]
        OT = [keep.tile([P, 4, DH], F32, name="ot0", tag="ot0")]
        arena = keep.tile([P, 8, 4, RANK], BF16, name="arena", tag="arena", align_bytes=64)
        ZR = keep.tile([P, NR, CH], F32, name="zr", tag="zr")
        QR = keep.tile([P, NR, CH], F32, name="qr", tag="qr")
        GT = keep.tile([P, NG, 2, CH], F32, name="gt", tag="gt")
        TQ = keep.tile([P, 4, 4, P], F32, name="tq", tag="tq")

        def load_x(c, slot, halves):
            for h in halves:
                for op in range(2):
                    nc.sync.dma_start(
                        out=arena[:, slot + op, 2 * h : 2 * h + 2, :], in_=x_views[op][:, 4 * c + 2 * h : 4 * c + 2 * h + 2, :]
                    )

        def load_w1(dt):
            for op in range(2):
                nc.sync.dma_start(out=arena[:, op, dt, :], in_=w_views[op][:, dt, :])

        def load_wg(g, slot):
            for op in range(2):
                nc.sync.dma_start(out=arena[:, slot + op, :, :], in_=w_views[op][:, 4 * g : 4 * g + 4, :])

        def load_state(c, a, b):
            nc.sync.dma_start(out=ST[c][:, :, a:b], in_=st_view[:, 4 * c : 4 * c + 4, a:b])

        wslot = {0: 0, 1: 4, 2: 6, 3: 0}
        xslot = {0: 2, 1: 2}
        load_w1(0)
        load_x(0, 2, [0, 1])
        load_w1(1)
        load_w1(2)
        load_w1(3)
        if LORD == 0:
            load_wg(1, 4)
            load_state(0, 0, 2 * CH)
            load_wg(2, 6)
        elif LORD == 1:
            load_wg(1, 4)
            load_state(0, 0, CH)
            load_wg(2, 6)
            load_state(0, CH, 2 * CH)
            load_state(0, 2 * CH, 3 * CH)
        else:
            load_wg(1, 4)
            load_wg(2, 6)
            load_state(0, 0, 2 * CH)
            load_state(0, 2 * CH, 3 * CH)

        ident = const.tile([P, P], F32, name="ident", tag="ident")
        make_identity(nc, ident[:])
        identb = const.tile([P, P], BF16, name="identb", tag="identb")
        make_identity(nc, identb[:])
        zero = const.tile([P, 1], F32, name="zero", tag="zero")
        nc.vector.memset(zero[:], 0.0)
        am = const.tile([P, 2 * 4 * NPART], F32, name="am", tag="am")
        nc.vector.memset(am[:], 0.0)
        fac = const.tile([P, 3, 8], F32, name="fac", tag="fac")
        sg = const.tile([P, 2], F32, name="sg", tag="sg")
        cst = const.tile([P, 2], F32, name="cst", tag="cst")
        brow32 = const.tile([P, P], F32, name="brow32", tag="brow32")
        bias = const.tile([P, 2 * NDT], F32, name="bias", tag="bias")
        nc.scalar.activation(out=sg[:, 0:1], in_=zero[:], func=ACT.Sigmoid)

        if WARM:
            wt = pst.tile([P, 4, P], F32, name="tp", tag="tp")
            for n in range(WARM):
                nc.tensor.matmul(out=wt[:, n % 4, :], lhsT=identb[:], rhs=identb[:], start=True, stop=True)

        wloc = {}
        xloc = {}

        def new_job(name, srcs, big, codes=None, scales=None, off=0):
            n = len(srcs)
            if codes is None:
                codes = keep.tile([P, n * P], U32, name="c" + name, tag="c" + name, align_bytes=64)
                scales = keep.tile([P, n * P], U8, name="s" + name, tag="s" + name, align_bytes=64)
            gtag = "grL" if big else "grS"
            grouped = grp.tile([P, n * P * 4], BF16, name=gtag, tag=gtag, align_bytes=64, bufs=(1 if big else GRSB))
            g32 = grouped[:].bitcast(F32).rearrange("p (s r u) -> p s r u", s=n, u=2)
            return {"srcs": srcs, "codes": codes, "scales": scales, "grouped": grouped, "g32": g32, "off": off, "n": n}

        def piece(job, k, eng):
            bank = pst.tile([P, 2, 2, P], F32, name="tp", tag="tp")
            for s in range(2):
                words = job["srcs"][2 * k + s].bitcast(F32)
                for u in range(2):
                    nc.tensor.transpose(bank[:, s, u, :], words[:, u : RANK // 2 : 2], ident[:])
            src = bank[:].rearrange("p s u r -> p s r u")
            dst = job["g32"][:, 2 * k : 2 * k + 2]
            if eng == "v":
                nc.vector.tensor_copy(out=dst, in_=src)
            else:
                nc.scalar.copy(out=dst, in_=src)

        def quant(job):
            a, n = job["off"], job["n"] * P
            nc.vector.quantize_mx(
                out=job["codes"][:, a : a + n].bitcast(FP8X4), scales=job["scales"][:, a : a + n], in_=job["grouped"][:]
            )

        def w_job(name, dts, big):
            srcs = []
            for dt in dts:
                for op in range(2):
                    srcs.append(arena[:, wslot[dt // 4] + op, dt % 4, :])
            job = new_job(name, srcs, big)
            for n, dt in enumerate(dts):
                for op in range(2):
                    wloc[(dt, op)] = (job, (2 * n + op) * P)
            return job

        accs = {}
        zTs = {}
        qTs = {}
        batch_of = {}
        bidx = {}
        for n, units in enumerate(BATCHES):
            for i in units:
                batch_of[i] = units
                bidx[i] = n

        def zs(i):
            return ZR[:, i % NR, :]

        def qs(i):
            return QR[:, i % NR, :]

        def mx(i):
            c, dt = i // NDT, i % NDT
            acc = psa.tile([P, CH], F32, name="acc", tag="acc")
            for op in range(2):
                wj, wo = wloc[(dt, op)]
                xj, xo = xloc[(c, op)]
                nc.tensor.matmul_mx(
                    out=acc[:],
                    lhsT=wj["codes"][:, wo : wo + P].bitcast(FP8X4),
                    lhsT_scale=wj["scales"][:, wo : wo + P],
                    rhs=xj[0][:, xo : xo + CH].bitcast(FP8X4),
                    rhs_scale=xj[1][:, xo : xo + CH],
                    start=(op == 0),
                    stop=(op == 1),
                )
            accs[i] = acc

        def act(i):
            dt = i % NDT
            nc.scalar.activation(out=zs(i), in_=accs[i][:], func=ACT.Sigmoid, bias=bias[:, dt : dt + 1], scale=1.0)
            nc.scalar.activation(
                out=qs(i), in_=accs[i][:], func=ACT.Tanh, bias=bias[:, NDT + dt : NDT + dt + 1], scale=1.0
            )
            if tsrc(i) == "s":
                nc.scalar.activation(
                    out=GT[:, bidx[i] % NG, batch_of[i].index(i), :], in_=zs(i), func=ACT.Identity,
                    scale=cst[:, 0:1], bias=cst[:, 1:2],
                )

        def tsrc(i):
            return TSRC[bidx[i] % len(TSRC)]

        pend = []

        def gq(i, late=False):
            units = batch_of[i]
            if i != units[-1]:
                return
            if (tsrc(i) == "v" or i in QV) and not late:
                pend.append(i)
                return
            a, n = units[0] % NR, len(units)
            g = GT[:, bidx[i] % NG, 0:n, :]
            if tsrc(i) != "s":
                eng = nc.vector if (tsrc(i) == "v" or i in QV) else nc.gpsimd
                eng.tensor_scalar(
                    out=g, in0=ZR[:, a : a + n, :], scalar1=cst[:, 0:1], scalar2=cst[:, 1:2], op0=ALU.mult, op1=ALU.add
                )
            eng2 = nc.vector if i in QV else nc.gpsimd
            eng2.tensor_tensor(out=QR[:, a : a + n, :], in0=g, in1=QR[:, a : a + n, :], op=ALU.mult)

        def flush():
            while pend:
                gq(pend.pop(0), True)

        def tt(i):
            zT = pst.tile([P, 4, P], F32, name="tp", tag="tp")
            qT = pst.tile([P, 4, P], F32, name="tp", tag="tp")
            for jj in range(4):
                nc.tensor.transpose(zT[:, jj, :], zs(i)[:, jj * P : (jj + 1) * P], ident[:])
            for jj in range(4):
                nc.tensor.transpose(qT[:, jj, :], qs(i)[:, jj * P : (jj + 1) * P], ident[:])
            zTs[i] = zT
            qTs[i] = qT

        def vv(i):
            c, dt = i // NDT, i % NDT
            cols = slice(dt * P, (dt + 1) * P)
            nc.vector.tensor_tensor(out=OT[c][:, :, cols], in0=zTs[i][:], in1=ST[c][:, :, cols], op=ALU.mult)
            nc.vector.tensor_tensor(out=OT[c][:, :, cols], in0=qTs[i][:], in1=OT[c][:, :, cols], op=ALU.add)

        sTs = {}
        oTs = {}

        def xts(i):
            c, dt = i // NDT, i % NDT
            sT = pst.tile([P, 4, P], BF16, name="tp", tag="tp")
            for jj in range(4):
                nc.tensor.transpose(sT[:, jj, :], ST[c][:, jj, dt * P : (dt + 1) * P], identb[:])
            sTs[i] = sT

        def xvt(i):
            nc.vector.tensor_tensor(
                out=TQ[:, i % 4], in0=zs(i).rearrange("p (j r) -> p j r", j=4), in1=sTs[i][:], op=ALU.mult
            )

        def xtt(i):
            oT = pst.tile([P, 4, P], F32, name="tp", tag="tp")
            for jj in range(4):
                nc.tensor.matmul(
                    out=oT[:, jj, :], lhsT=TQ[:, i % 4, jj, :], rhs=ident[:], is_transpose=True, start=True, stop=False
                )
                nc.tensor.matmul(
                    out=oT[:, jj, :], lhsT=qs(i)[:, jj * P : (jj + 1) * P], rhs=ident[:], is_transpose=True,
                    start=False, stop=True,
                )
            oTs[i] = oT

        def xev(i):
            c, dt = i // NDT, i % NDT
            if VEVAC <= i < VEND and i % VMOD == 0:
                nc.vector.tensor_copy(out=OT[c][:, :, dt * P : (dt + 1) * P], in_=oTs[i][:])
            else:
                nc.scalar.copy(out=OT[c][:, :, dt * P : (dt + 1) * P], in_=oTs[i][:])

        def amax(c, jj, a, b, part):
            col = (c * 4 + jj) * NPART + part
            nc.vector.tensor_reduce(
                out=am[:, col : col + 1], in_=OT[c][:, jj, a:b], axis=AX.X, op=ALU.max, apply_absolute_value=True
            )

        def fin(c):
            sl = slice(4 * c, 4 * c + 4)
            nc.vector.tensor_reduce(
                out=fac[:, 0, sl],
                in_=am[:, c * 4 * NPART : (c + 1) * 4 * NPART].rearrange("p (j n) -> p j n", n=NPART),
                axis=AX.X,
                op=ALU.max,
            )
            nc.vector.reciprocal(out=fac[:, 1, sl], in_=fac[:, 0, sl])
            nc.vector.tensor_scalar(out=fac[:, 2, sl], in0=fac[:, 1, sl], scalar1=448.0, scalar2=None, op0=ALU.mult)

        f8s = {}

        def cast(c, jj, a, b, eng):
            j = 4 * c + jj
            if j not in f8s:
                f8s[j] = work.tile([P, DH], FP8, name="f8", tag="f8", bufs=6)
            r = fac[:, 2, j : j + 1]
            if eng == "v":
                nc.vector.tensor_scalar(
                    out=f8s[j][:, a:b], in0=OT[c][:, jj, a:b], scalar1=r, scalar2=None, op0=ALU.mult, saturate=False
                )
            else:
                nc.scalar.activation(
                    out=f8s[j][:, a:b], in_=OT[c][:, jj, a:b], func=ACT.Identity, scale=r, bias=zero[:, 0:1],
                    saturate=False,
                )

        def store1(c, jj):
            j = 4 * c + jj
            nc.sync.dma_start(out=o1_view[:, j, :], in_=f8s[j][:].bitcast(U8))

        def store0(c, a, b):
            cols = slice(a, b)
            nc.sync.dma_start(out=o0_view[:, 4 * c : 4 * c + 4, cols], in_=OT[c][:, :, cols])

        xc = [keep.tile([P, 2 * CH], U32, name="xc%d" % c, tag="xc%d" % c, align_bytes=64) for c in range(2)]
        xs = [keep.tile([P, 2 * CH], U8, name="xs%d" % c, tag="xs%d" % c, align_bytes=64) for c in range(2)]
        for c in range(2):
            for op in range(2):
                xloc[(c, op)] = ((xc[c], xs[c]), op * CH)

        def x_half(c, op, h):
            srcs = [arena[:, xslot[c] + op, 2 * h + r, :] for r in range(2)]
            return new_job("x", srcs, False, xc[c], xs[c], op * CH + h * 2 * P)

        jw0 = w_job("w0", [0], False)
        piece(jw0, 0, "s")
        ja = x_half(0, 0, 0)
        piece(ja, 0, "v")
        jb = x_half(0, 1, 0)
        piece(jb, 0, "s")
        quant(jw0)
        jc = x_half(0, 0, 1)
        piece(jc, 0, "v")
        quant(ja)
        nc.vector.tensor_copy(out=brow32[:], in_=brow[:])
        jd = x_half(0, 1, 1)
        piece(jd, 0, "s")
        quant(jb)
        bT = pst.tile([P, P], F32, name="tp", tag="tp")
        nc.tensor.transpose(bT[:], brow32[:], ident[:])
        quant(jc)
        nc.vector.tensor_copy(out=bias[:], in_=bT[:, 0 : 2 * NDT])
        quant(jd)
        nc.scalar.activation(out=sg[:, 0:1], in_=zt[:], func=ACT.Sigmoid)
        nc.scalar.activation(out=sg[:, 1:2], in_=nt[:], func=ACT.Sigmoid)
        nc.vector.tensor_scalar(out=cst[:, 0:1], in0=sg[:, 0:1], scalar1=-1.0, scalar2=None, op0=ALU.mult)
        nc.vector.tensor_tensor(out=cst[:, 1:2], in0=sg[:, 0:1], in1=sg[:, 1:2], op=ALU.add)

        jobs = {}

        def get_job(name):
            if name not in jobs:
                if name[0] == "w":
                    p = int(name[1:])
                    jobs[name] = w_job("p" + name, [1] if p == 0 else [2 * p, 2 * p + 1], False)
                else:
                    op = int(name[1:])
                    srcs = [arena[:, xslot[1] + op, r, :] for r in range(4)]
                    jobs[name] = new_job("x", srcs, False, xc[1], xs[1], op * CH)
            return jobs[name]

        order = ["w%d" % p for p in range(0, 8)] + ["x0", "x1"]
        pieces_done = [0]
        quants_done = [0]

        def prep_pieces(n):
            while pieces_done[0] < min(n, len(order)):
                j = get_job(order[pieces_done[0]])
                for kk in range(len(j["srcs"]) // 2):
                    piece(j, kk, PIECE_ENG[(2 * pieces_done[0] + kk) % len(PIECE_ENG)])
                pieces_done[0] += 1

        def prep_quants(n):
            while quants_done[0] < min(n, pieces_done[0]):
                quant(get_job(order[quants_done[0]]))
                quants_done[0] += 1

        def front(i):
            mx(i)
            act(i)
            gq(i)

        amax_at = {}
        for jj in range(4):
            amax_at[A0 + jj] = [(0, jj, 0, 1024, 0)]
            amax_at[16 + jj] = [(0, jj, 1024, 2048, 1)]
            amax_at[20 + jj] = [(1, jj, 0, 512, 0)]
            amax_at[24 + jj] = [(1, jj, 512, 1024, 4)]
        amax_at[28] = [(1, 0, 1024, 1536, 1)]
        amax_at[29] = [(1, 1, 1024, 1536, 1)]
        amax_at[30] = [(1, 2, 1024, 1536, 1), (1, 3, 1024, 1536, 1)] + [(1, jj, 1536, 1920, 2) for jj in range(4)]
        amax_at[31] = [(1, jj, 1920, 2048, 3) for jj in range(4)]

        def after(s):
            if s % 8 == 7 and s != NU - 1:
                store0(s // NDT, (s % NDT - 7) * P, (s % NDT + 1) * P)
            if s == NU - 5:
                store0(1, (s % NDT - 3) * P, (s % NDT + 1) * P)
            if s in (NU - 3, NU - 1):
                store0(1, (s % NDT - 1) * P, (s % NDT + 1) * P)
            for c, jj, a, b, part in amax_at.get(s, []):
                amax(c, jj, a, b, part)
            if s == 19:
                fin(0)
            if CAST0 <= s < CAST0 + 8:
                jj, h = (s - CAST0) // 2, (s - CAST0) % 2
                cast(0, jj, h * 1024, (h + 1) * 1024, C0ENG[(s - CAST0) % len(C0ENG)])
                if h == 1:
                    store1(0, jj)

        prep_pieces(P0)
        prep_quants(1)
        fnext = [0]
        for kp in range(-LP, NU // 2):
            target = kp + (LP if kp < KL else LP2)
            f = fnext[0]
            while fnext[0] <= min(target, NU // 2 - 1):
                f = fnext[0]
                prep_quants(f + QA)
                flush()
                mx(2 * f)
                mx(2 * f + 1)
                act(2 * f)
                gq(2 * f)
                act(2 * f + 1)
                gq(2 * f + 1)
                if f == 1:
                    load_wg(3, 0)
                    load_state(0, 2 * CH, 4 * CH)
                if f == 2:
                    load_x(1, 2, [0, 1])
                    load_state(1, 0, 2 * CH)
                    load_state(1, 2 * CH, 4 * CH)
                fnext[0] += 1
            if fnext[0] >= NU // 2:
                flush()
            md = kp + 1
            if 0 <= md < NU // 2 and 2 * md >= XFROM:
                xts(2 * md)
                xts(2 * md + 1)
                xvt(2 * md)
                xvt(2 * md + 1)
            if kp >= 0:
                if 2 * kp == NDT:
                    OT.append(keep.tile([P, 4, DH], F32, name="arena", tag="arena", align_bytes=64))
                for s in (2 * kp, 2 * kp + 1):
                    if s >= XFROM:
                        xtt(s)
                    else:
                        tt(s)
                for s in (2 * kp, 2 * kp + 1):
                    if s >= XFROM:
                        xev(s)
                    else:
                        vv(s)
            prep_pieces(min(f + PA, P0 + 1 + PR * f))
            if kp >= 0:
                after(2 * kp)
                after(2 * kp + 1)

        fin(1)
        for jj in range(4):
            cast(1, jj, 0, VCAST, "v")
            cast(1, jj, VCAST, DH, "s")
            store1(1, jj)
